import numpy as np
import ml_dtypes


def mxq(x, axis, fmt="e4m3"):
    dtype, down = {"e4m3": (ml_dtypes.float8_e4m3fn, 7), "e5m2": (ml_dtypes.float8_e5m2, 14)}[fmt]
    v = np.moveaxis(np.asarray(x, np.float32).astype(ml_dtypes.bfloat16).astype(np.float64), axis, -1)
    blocks = v.reshape(v.shape[:-1] + (-1, 32))
    amax = np.abs(blocks).max(-1, keepdims=True)
    byte = np.maximum(np.where(amax > 0, np.frexp(amax)[1] - 1 + 127, 0) - down, 1)
    scale = np.exp2(byte - 127.0)
    codes = (blocks / scale).astype(np.float32).astype(dtype).astype(np.float64)
    return np.moveaxis((codes * scale).reshape(v.shape), -1, axis)


WIDE = False


def mx_kscale(k):
    if not WIDE:
        return np.ones(k)
    levels = np.array([10, -10, 5, -5, 0])
    a = np.random.permutation(np.resize(levels, k // 512 * 4)).reshape(k // 512, 4)
    idx = np.arange(k)
    return np.exp2(a[idx // 512, idx % 128 // 32])


BF16 = ml_dtypes.bfloat16


def bf(x):
    return np.asarray(x, np.float32).astype(BF16)


def f64(x):
    return np.asarray(x).astype(np.float64)


E2M1 = np.array([0.0, 0.5, 1.0, 1.5, 2.0, 3.0, 4.0, 6.0, -0.0, -0.5, -1.0, -1.5, -2.0, -3.0, -4.0, -6.0])


def pack_weight(w, fmt):
    k, n = w.shape
    w = f64(bf(w)).reshape(k // 32, 32, n)
    amax = np.abs(w).max(1)
    if fmt == "e4m3":
        byte = np.frexp(amax)[1] - 1 + 127 - 7
    else:
        mant, ex = np.frexp(amax / 6.0)
        byte = np.where(mant > 0.5, ex, ex - 1) + 127
    byte = np.clip(np.where(amax > 0, byte, 1), 1, 254)
    scaled = (w * np.exp2(127.0 - byte)[:, None, :]).reshape(k, n).astype(np.float32)
    by_word = np.ascontiguousarray(scaled.reshape(k // 512, 128, 4, n).transpose(0, 1, 3, 2))
    if fmt == "e4m3":
        words = by_word.astype(ml_dtypes.float8_e4m3fn).view(np.uint8)
    else:
        c = by_word.astype(ml_dtypes.float4_e2m1fn).view(np.uint8) & 0xF
        words = c[..., 0::2] | (c[..., 1::2] << 4)
    return np.ascontiguousarray(words), np.ascontiguousarray(byte.astype(np.uint8).reshape(k // 512, 16, n))


def unpack_weight(words, scales, fmt):
    g, p, n, _ = words.shape
    if fmt == "e4m3":
        vals = np.ascontiguousarray(words).view(ml_dtypes.float8_e4m3fn).astype(np.float64)
    else:
        nib = np.empty((g, p, n, 4), np.uint8)
        nib[..., 0::2] = words & 0xF
        nib[..., 1::2] = words >> 4
        vals = E2M1[nib]
    vals = vals * np.repeat(np.exp2(scales.astype(np.float64) - 127.0), 8, axis=1)[..., None]
    return vals.transpose(0, 1, 3, 2).reshape(g * 512, n)


B, IN, H = 128, 2048, 1536
G = 4 * H
EPS = 1e-5
FMT = "e4m3"


def _layernorm(v, gamma, beta):
    mean = np.mean(v, axis=-1, keepdims=True)
    var = np.mean(np.square(v - mean), axis=-1, keepdims=True)
    return (v - mean) / np.sqrt(var + EPS) * gamma + beta


def sigmoid(v):
    return 1.0 / (1.0 + np.exp(-v))


def setup_inputs():
    s, t = mx_kscale(IN), mx_kscale(H)
    x = bf(np.random.standard_normal((B, IN)) * s)
    h_prev = bf(np.random.standard_normal((B, H)) * t)
    c_prev = bf(np.random.standard_normal((B, H)))
    W_ih_words, W_ih_scales = pack_weight(np.random.standard_normal((IN, G)) / np.sqrt(IN) / s[:, None], FMT)
    W_hh_words, W_hh_scales = pack_weight(np.random.standard_normal((H, G)) / np.sqrt(H) / t[:, None], FMT)
    return {
        "x": x,
        "h_prev": h_prev,
        "c_prev": c_prev,
        "W_ih_words": W_ih_words,
        "W_ih_scales": W_ih_scales,
        "W_hh_words": W_hh_words,
        "W_hh_scales": W_hh_scales,
        "gamma_ih": bf(1.0 + 0.2 * np.random.standard_normal(G)),
        "beta_ih": bf(0.3 * np.random.standard_normal(G)),
        "gamma_hh": bf(1.0 + 0.2 * np.random.standard_normal(G)),
        "beta_hh": bf(0.3 * np.random.standard_normal(G)),
        "gamma_c": bf(1.0 + 0.2 * np.random.standard_normal(H)),
        "beta_c": bf(0.3 * np.random.standard_normal(H)),
    }


def reference(x, h_prev, c_prev, W_ih_words, W_ih_scales, W_hh_words, W_hh_scales, gamma_ih, beta_ih, gamma_hh, beta_hh, gamma_c, beta_c):
    a_ih = mxq(f64(x), 1, "e4m3") @ unpack_weight(W_ih_words, W_ih_scales, FMT)
    a_hh = mxq(f64(h_prev), 1, "e4m3") @ unpack_weight(W_hh_words, W_hh_scales, FMT)
    gates_ih = _layernorm(a_ih, f64(gamma_ih), f64(beta_ih))
    gates_hh = _layernorm(a_hh, f64(gamma_hh), f64(beta_hh))
    gates = gates_ih + gates_hh
    i_g, f_g, g_g, o_g = np.split(gates, 4, axis=1)
    i_t = sigmoid(i_g)
    f_t = sigmoid(f_g)
    g_t = np.tanh(g_g)
    o_t = sigmoid(o_g)
    c_t = f_t * f64(c_prev) + i_t * g_t
    h_t = o_t * np.tanh(_layernorm(c_t, f64(gamma_c), f64(beta_c)))
    return (h_t, c_t)

@@ -1,0 +1,297 @@
+from contextlib import ExitStack
+
+import concourse.mybir as mybir
+from concourse.masks import make_identity
+
+F32 = mybir.dt.float32
+BF16 = mybir.dt.bfloat16
+I32 = mybir.dt.int32
+U32 = mybir.dt.uint32
+U8 = mybir.dt.uint8
+FP8X4 = mybir.dt.float8_e4m3fn_x4
+ALU = mybir.AluOpType
+ACT = mybir.ActivationFunctionType
+
+P = 128
+PACK = 4
+K_PASS = P * PACK
+BANK = 512
+IN = 2048
+H = 1536
+GATES = 4
+G = GATES * H
+GATE_I, GATE_F, GATE_G, GATE_O = 0, 1, 2, 3
+BANKS_PER_GATE = H // BANK
+TILES_PER_GATE = H // P
+EPS = 1e-5
+SPREAD_RUN = 4
+SCALE_CUTS = 2
+SLAB_BUFS = 8
+
+FLOPS = 2 * P * (IN + H) * G
+
+
+def quantise_rows(nc, keep, turned, ident_f32, raw, groups, label):
+    pairs = raw[:].bitcast(F32)
+    grouped = keep.tile([P, groups, P, PACK], BF16, name=label + "_grouped", align_bytes=64)
+    codes = keep.tile([P, groups, P], U32, name=label + "_codes", align_bytes=64)
+    scales = keep.tile([P, groups, P], U8, name=label + "_scales", align_bytes=64)
+    half = K_PASS // 2
+    for g in range(groups):
+        flipped = turned.tile([P, 2, P], F32, name="flipped", tag="turned")
+        for u in range(2):
+            nc.tensor.transpose(flipped[:, u, :], pairs[:, g * half + u : (g + 1) * half : 2], ident_f32[:])
+        nc.vector.tensor_copy(
+            out=grouped[:, g].rearrange("p b t -> p (b t)").bitcast(F32).rearrange("p (b u) -> p b u", u=2),
+            in_=flipped[:].rearrange("p u b -> p b u"),
+        )
+    for g in range(groups):
+        nc.vector.quantize_mx(
+            out=codes[:, g, :].bitcast(FP8X4),
+            scales=scales[:, g, :],
+            in_=grouped[:, g].rearrange("p b t -> p (b t)"),
+        )
+    return codes, scales
+
+
+def load_scale_planes(nc, keep, scales, groups, label):
+    planes = keep.tile([P, G], U8, name=label, align_bytes=64)
+    plane_words = planes[:].bitcast(I32)
+    nc.vector.memset(plane_words, 0)
+    source = scales.bitcast(I32)
+    width = G // 4 // SCALE_CUTS
+    for quadrant in range(4):
+        for cut in range(SCALE_CUTS):
+            cols = slice(cut * width, (cut + 1) * width)
+            nc.sync.dma_start(
+                out=plane_words[32 * quadrant : 32 * quadrant + 4 * groups, cols],
+                in_=source[:, 4 * quadrant : 4 * quadrant + 4, cols],
+            )
+    return planes
+
+
+def spread(nc, turned, ident, columns, first, dest):
+    for start in range(0, TILES_PER_GATE, SPREAD_RUN):
+        bank = turned.tile([P, SPREAD_RUN, P], columns.dtype, name="spread_bank", tag="turned")
+        for m in range(SPREAD_RUN):
+            col = first + start + m
+            nc.tensor.transpose(bank[:, m, :], columns[:, col : col + 1].to_broadcast([P, P]), ident[:])
+        nc.scalar.copy(
+            out=dest[:, start * P : (start + SPREAD_RUN) * P],
+            in_=bank[:].rearrange("p m n -> p (m n)"),
+        )
+
+
+def project_gate(nc, slabs, sums, words, planes, codes, code_scales, groups, gate, dest, stats):
+    first = gate * H
+    banks = [sums.tile([P, BANK], F32, name="bank%d" % j, tag="sum") for j in range(BANKS_PER_GATE)]
+    for g in range(groups):
+        slab = slabs.tile([P, H], U32, name="slab", align_bytes=64)
+        nc.sync.dma_start(
+            out=slab[:].bitcast(I32),
+            in_=words[g, :, first : first + H, :].rearrange("p n t -> p (n t)").bitcast(I32),
+        )
+        for j in range(BANKS_PER_GATE):
+            nc.tensor.matmul_mx(
+                out=banks[j][:],
+                lhsT=codes[:, g, :].bitcast(FP8X4),
+                lhsT_scale=code_scales[:, g, :],
+                rhs=slab[:, j * BANK : (j + 1) * BANK].bitcast(FP8X4),
+                rhs_scale=planes[4 * g : P, first + j * BANK : first + (j + 1) * BANK],
+                start=(g == 0),
+                stop=(g == groups - 1),
+            )
+    for j in range(BANKS_PER_GATE):
+        cols = slice(first + j * BANK, first + (j + 1) * BANK)
+        nc.scalar.copy(out=dest[:, cols], in_=banks[j][:])
+        nc.vector.bn_stats(out=stats[:, gate * BANKS_PER_GATE + j, :], in_=dest[:, cols])
+
+
+def inverse_root(nc, keep, minus_half, total, share, label):
+    shifted = keep.tile([P, 1], F32, name=label + "_shifted")
+    nc.gpsimd.tensor_scalar(out=shifted[:], in0=total, scalar1=share, scalar2=EPS, op0=ALU.mult, op1=ALU.add)
+    rstd = keep.tile([P, 1], F32, name=label + "_rstd")
+    nc.gpsimd.tensor_tensor(out=rstd[:], in0=shifted[:], in1=minus_half[:], op=ALU.pow)
+    return rstd
+
+
+def mean_and_rstd(nc, keep, minus_half, stats, label):
+    mean_var = keep.tile([P, 2], F32, name=label + "_mean_var")
+    nc.vector.bn_aggr(out=mean_var[:], in_=stats[:].rearrange("p c s -> p (c s)"))
+    rstd = inverse_root(nc, keep, minus_half, mean_var[:, 1:2], 1.0, label)
+    return mean_var[:, 0:1], rstd[:]
+
+
+def centre_and_gain(nc, values, mean, gain):
+    nc.vector.scalar_tensor_tensor(out=values, in0=values, scalar=mean, in1=gain, op0=ALU.subtract, op1=ALU.mult)
+
+
+def scale_and_add(nc, values, rstd, addend):
+    nc.vector.scalar_tensor_tensor(out=values, in0=values, scalar=rstd, in1=addend, op0=ALU.mult, op1=ALU.add)
+
+
+def tile_layernormlstmcell_w_kernel(
+    tc,
+    x,
+    h_prev,
+    c_prev,
+    W_ih_words,
+    W_ih_scales,
+    W_hh_words,
+    W_hh_scales,
+    gamma_ih,
+    beta_ih,
+    gamma_hh,
+    beta_hh,
+    gamma_c,
+    beta_c,
+    out_0,
+    out_1,
+):
+    nc = tc.nc
+    x_groups = IN // K_PASS
+    h_groups = H // K_PASS
+    vector_tiles = G // P
+
+    with ExitStack() as stack:
+        stack.enter_context(tc.manual_schedule())
+        keep = stack.enter_context(tc.tile_pool(name="keep", bufs=1))
+        slabs = stack.enter_context(tc.tile_pool(name="slabs", bufs=SLAB_BUFS))
+        sums = stack.enter_context(tc.psum_pool(name="sums", bufs=2 * BANKS_PER_GATE))
+        turned = stack.enter_context(tc.psum_pool(name="turned", bufs=2))
+
+        h_raw = keep.tile([P, H], BF16, name="h_raw")
+        nc.sync.dma_start(out=h_raw[:], in_=h_prev)
+        x_raw = keep.tile([P, IN], BF16, name="x_raw")
+        nc.sync.dma_start(out=x_raw[:], in_=x)
+        hh_planes = load_scale_planes(nc, keep, W_hh_scales, h_groups, "hh_planes")
+        ih_planes = load_scale_planes(nc, keep, W_ih_scales, x_groups, "ih_planes")
+
+        gain_rows = keep.tile([P, P], BF16, name="gain_rows")
+        beta_rows = keep.tile([P, P], BF16, name="beta_rows")
+        nc.vector.memset(gain_rows[:], 0.0)
+        nc.vector.memset(beta_rows[:], 0.0)
+        gamma_hh_at, gamma_ih_at = 0, vector_tiles
+        gamma_c_at, beta_c_at = 2 * vector_tiles, 2 * vector_tiles + TILES_PER_GATE
+        for vector, rows, at in (
+            (gamma_hh, gain_rows, gamma_hh_at),
+            (beta_hh, beta_rows, 0),
+            (beta_ih, beta_rows, vector_tiles),
+            (gamma_c, gain_rows, gamma_c_at),
+            (beta_c, gain_rows, beta_c_at),
+            (gamma_ih, gain_rows, gamma_ih_at),
+        ):
+            as_rows = vector.rearrange("(r n) -> r n", n=P)
+            nc.scalar.dma_start(out=rows[at : at + as_rows.shape[0], :], in_=as_rows)
+
+        ident_f32 = keep.tile([P, P], F32, name="ident_f32")
+        make_identity(nc, ident_f32[:])
+        ident_bf16 = keep.tile([P, P], BF16, name="ident_bf16")
+        make_identity(nc, ident_bf16[:])
+        minus_half = keep.tile([P, 1], F32, name="minus_half")
+        nc.gpsimd.memset(minus_half[:], -0.5)
+        warm = keep.tile([P, 1], F32, name="warm")
+        nc.vector.memset(warm[:], 0.0)
+        nc.scalar.activation(out=warm[:], in_=warm[:], func=ACT.Sigmoid)
+
+        h_codes, h_scales = quantise_rows(nc, keep, turned, ident_f32, h_raw, h_groups, "h")
+        x_codes, x_scales = quantise_rows(nc, keep, turned, ident_f32, x_raw, x_groups, "x")
+
+        gain_columns = keep.tile([P, P], BF16, name="gain_columns")
+        beta_columns = keep.tile([P, P], BF16, name="beta_columns")
+        for rows, columns in ((gain_rows, gain_columns), (beta_rows, beta_columns)):
+            flipped_rows = turned.tile([P, P], BF16, name="flipped_rows", tag="turned")
+            nc.tensor.transpose(flipped_rows[:], rows[:], ident_bf16[:])
+            nc.vector.tensor_copy(out=columns[:], in_=flipped_rows[:])
+        beta_sum_columns = keep.tile([P, vector_tiles], F32, name="beta_sum_columns")
+        nc.vector.tensor_add(
+            out=beta_sum_columns[:],
+            in0=beta_columns[:, 0:vector_tiles],
+            in1=beta_columns[:, vector_tiles : 2 * vector_tiles],
+        )
+
+        gain_hh = keep.tile([P, G], BF16, name="gain_hh")
+        gain_ih = keep.tile([P, G], BF16, name="gain_ih")
+        beta_sum = keep.tile([P, G], F32, name="beta_sum")
+        gain_c = keep.tile([P, H], BF16, name="gain_c")
+        bias_c = keep.tile([P, H], BF16, name="bias_c")
+        spread(nc, turned, ident_bf16, gain_columns, gamma_c_at, gain_c[:])
+        spread(nc, turned, ident_bf16, gain_columns, beta_c_at, bias_c[:])
+
+        rest = keep.tile([P, G], F32, name="rest")
+        hh_stats = keep.tile([P, G // BANK, 6], F32, name="hh_stats")
+        for gate in range(GATES):
+            cols = slice(gate * H, (gate + 1) * H)
+            spread(nc, turned, ident_bf16, gain_columns, gamma_hh_at + gate * TILES_PER_GATE, gain_hh[:, cols])
+            spread(nc, turned, ident_f32, beta_sum_columns, gate * TILES_PER_GATE, beta_sum[:, cols])
+            project_gate(nc, slabs, sums, W_hh_words, hh_planes, h_codes, h_scales, h_groups, gate, rest, hh_stats)
+
+        mean_hh, rstd_hh = mean_and_rstd(nc, keep, minus_half, hh_stats, "hh")
+        for gate in range(GATES):
+            cols = slice(gate * H, (gate + 1) * H)
+            centre_and_gain(nc, rest[:, cols], mean_hh, gain_hh[:, cols])
+        for gate in range(GATES):
+            cols = slice(gate * H, (gate + 1) * H)
+            scale_and_add(nc, rest[:, cols], rstd_hh, beta_sum[:, cols])
+
+        gates = keep.tile([P, G], F32, name="gates")
+        ih_stats = keep.tile([P, G // BANK, 6], F32, name="ih_stats")
+        for gate in range(GATES):
+            cols = slice(gate * H, (gate + 1) * H)
+            spread(nc, turned, ident_bf16, gain_columns, gamma_ih_at + gate * TILES_PER_GATE, gain_ih[:, cols])
+            project_gate(nc, slabs, sums, W_ih_words, ih_planes, x_codes, x_scales, x_groups, gate, gates, ih_stats)
+        c_old = keep.tile([P, H], BF16, name="c_old")
+        nc.sync.dma_start(out=c_old[:], in_=c_prev)
+
+        mean_ih, rstd_ih = mean_and_rstd(nc, keep, minus_half, ih_stats, "ih")
+
+        def block(gate):
+            return gates[:, gate * H : (gate + 1) * H]
+
+        def centre(gate):
+            centre_and_gain(nc, block(gate), mean_ih, gain_ih[:, gate * H : (gate + 1) * H])
+
+        def finish(gate, func):
+            scale_and_add(nc, block(gate), rstd_ih, rest[:, gate * H : (gate + 1) * H])
+            nc.scalar.activation(out=block(gate), in_=block(gate), func=func)
+
+        centre(GATE_G)
+        centre(GATE_I)
+        finish(GATE_G, ACT.Tanh)
+        finish(GATE_I, ACT.Sigmoid)
+        centre(GATE_F)
+        finish(GATE_F, ACT.Sigmoid)
+
+        c_new = keep.tile([P, H], F32, name="c_new")
+        c_sum = keep.tile([P, 1], F32, name="c_sum")
+        nc.vector.tensor_mul(out=block(GATE_I), in0=block(GATE_I), in1=block(GATE_G))
+        nc.vector.tensor_mul(out=block(GATE_F), in0=block(GATE_F), in1=c_old[:])
+        nc.vector.scalar_tensor_tensor(
+            out=c_new[:], in0=block(GATE_I), scalar=1.0, in1=block(GATE_F), op0=ALU.mult, op1=ALU.add, accum_out=c_sum[:]
+        )
+        nc.sync.dma_start(out=out_1, in_=c_new[:])
+
+        mean_c = keep.tile([P, 1], F32, name="mean_c")
+        nc.vector.tensor_scalar_mul(out=mean_c[:], in0=c_sum[:], scalar1=1.0 / H)
+        squares = keep.tile([P, H], F32, name="squares")
+        square_sum = keep.tile([P, 1], F32, name="square_sum")
+        nc.scalar.activation(
+            out=squares[:], in_=c_new[:], func=ACT.Square, bias=mean_c[:], scale=-1.0, accum_out=square_sum[:]
+        )
+        rstd_c = inverse_root(nc, keep, minus_half, square_sum[:], 1.0 / H, "c")
+        centre(GATE_O)
+        finish(GATE_O, ACT.Sigmoid)
+
+        normed = keep.tile([P, H], F32, name="normed")
+        h_new = keep.tile([P, H], F32, name="h_new")
+        nc.vector.scalar_tensor_tensor(
+            out=normed[:], in0=c_new[:], scalar=mean_c[:], in1=gain_c[:], op0=ALU.subtract, op1=ALU.mult
+        )
+        for j in range(BANKS_PER_GATE):
+            cols = slice(j * BANK, (j + 1) * BANK)
+            scale_and_add(nc, normed[:, cols], rstd_c[:], bias_c[:, cols])
+            nc.scalar.activation(out=normed[:, cols], in_=normed[:, cols], func=ACT.Tanh)
+        for j in range(BANKS_PER_GATE):
+            cols = slice(j * BANK, (j + 1) * BANK)
+            nc.vector.tensor_mul(out=h_new[:, cols], in0=block(GATE_O)[:, cols], in1=normed[:, cols])
+            nc.sync.dma_start(out=out_0[:, cols], in_=h_new[:, cols])

@@ -24,9 +24,10 @@ GATE_I, GATE_F, GATE_G, GATE_O = 0, 1, 2, 3
 BANKS_PER_GATE = H // BANK
 TILES_PER_GATE = H // P
 EPS = 1e-5
-SPREAD_RUN = 4
+PIECE_TILES = BANK // P
+LATE_TILES = 2 * PIECE_TILES
 SCALE_CUTS = 2
-SLAB_BUFS = 8
+SLAB_BUFS = 10
 
 FLOPS = 2 * P * (IN + H) * G
 
@@ -38,7 +39,7 @@ def quantise_rows(nc, keep, turned, ident_f32, raw, groups, label):
     scales = keep.tile([P, groups, P], U8, name=label + "_scales", align_bytes=64)
     half = K_PASS // 2
     for g in range(groups):
-        flipped = turned.tile([P, 2, P], F32, name="flipped", tag="turned")
+        flipped = turned.tile([P, 2, P], F32, name="flipped", tag="wide")
         for u in range(2):
             nc.tensor.transpose(flipped[:, u, :], pairs[:, g * half + u : (g + 1) * half : 2], ident_f32[:])
         nc.vector.tensor_copy(
@@ -70,39 +71,33 @@ def load_scale_planes(nc, keep, scales, groups, label):
     return planes
 
 
-def spread(nc, turned, ident, columns, first, dest):
-    for start in range(0, TILES_PER_GATE, SPREAD_RUN):
-        bank = turned.tile([P, SPREAD_RUN, P], columns.dtype, name="spread_bank", tag="turned")
-        for m in range(SPREAD_RUN):
-            col = first + start + m
-            nc.tensor.transpose(bank[:, m, :], columns[:, col : col + 1].to_broadcast([P, P]), ident[:])
-        nc.scalar.copy(
-            out=dest[:, start * P : (start + SPREAD_RUN) * P],
-            in_=bank[:].rearrange("p m n -> p (m n)"),
-        )
+def spread(nc, bank, ident, columns, first):
+    for m in range(bank.shape[1]):
+        nc.tensor.transpose(bank[:, m, :], columns[:, first + m : first + m + 1].to_broadcast([P, P]), ident[:])
 
 
-def project_gate(nc, slabs, sums, words, planes, codes, code_scales, groups, gate, dest, stats):
+def multiply_slab(nc, slabs, words, planes, codes, code_scales, groups, gate, g, banks):
     first = gate * H
-    banks = [sums.tile([P, BANK], F32, name="bank%d" % j, tag="sum") for j in range(BANKS_PER_GATE)]
-    for g in range(groups):
-        slab = slabs.tile([P, H], U32, name="slab", align_bytes=64)
-        nc.sync.dma_start(
-            out=slab[:].bitcast(I32),
-            in_=words[g, :, first : first + H, :].rearrange("p n t -> p (n t)").bitcast(I32),
-        )
-        for j in range(BANKS_PER_GATE):
-            nc.tensor.matmul_mx(
-                out=banks[j][:],
-                lhsT=codes[:, g, :].bitcast(FP8X4),
-                lhsT_scale=code_scales[:, g, :],
-                rhs=slab[:, j * BANK : (j + 1) * BANK].bitcast(FP8X4),
-                rhs_scale=planes[4 * g : P, first + j * BANK : first + (j + 1) * BANK],
-                start=(g == 0),
-                stop=(g == groups - 1),
-            )
+    slab = slabs.tile([P, H], U32, name="slab", align_bytes=64)
+    nc.sync.dma_start(
+        out=slab[:].bitcast(I32),
+        in_=words[g, :, first : first + H, :].rearrange("p n t -> p (n t)").bitcast(I32),
+    )
     for j in range(BANKS_PER_GATE):
-        cols = slice(first + j * BANK, first + (j + 1) * BANK)
+        nc.tensor.matmul_mx(
+            out=banks[j][:],
+            lhsT=codes[:, g, :].bitcast(FP8X4),
+            lhsT_scale=code_scales[:, g, :],
+            rhs=slab[:, j * BANK : (j + 1) * BANK].bitcast(FP8X4),
+            rhs_scale=planes[4 * g : P, first + j * BANK : first + (j + 1) * BANK],
+            start=(g == 0),
+            stop=(g == groups - 1),
+        )
+
+
+def move_out(nc, banks, gate, dest, stats):
+    for j in range(BANKS_PER_GATE):
+        cols = slice(gate * H + j * BANK, gate * H + (j + 1) * BANK)
         nc.scalar.copy(out=dest[:, cols], in_=banks[j][:])
         nc.vector.bn_stats(out=stats[:, gate * BANKS_PER_GATE + j, :], in_=dest[:, cols])
 
@@ -157,7 +152,7 @@ def tile_layernormlstmcell_w_kernel(
         stack.enter_context(tc.manual_schedule())
         keep = stack.enter_context(tc.tile_pool(name="keep", bufs=1))
         slabs = stack.enter_context(tc.tile_pool(name="slabs", bufs=SLAB_BUFS))
-        sums = stack.enter_context(tc.psum_pool(name="sums", bufs=2 * BANKS_PER_GATE))
+        sums = stack.enter_context(tc.psum_pool(name="sums", bufs=BANKS_PER_GATE + 1))
         turned = stack.enter_context(tc.psum_pool(name="turned", bufs=2))
 
         h_raw = keep.tile([P, H], BF16, name="h_raw")
@@ -171,15 +166,17 @@ def tile_layernormlstmcell_w_kernel(
         beta_rows = keep.tile([P, P], BF16, name="beta_rows")
         nc.vector.memset(gain_rows[:], 0.0)
         nc.vector.memset(beta_rows[:], 0.0)
-        gamma_hh_at, gamma_ih_at = 0, vector_tiles
-        gamma_c_at, beta_c_at = 2 * vector_tiles, 2 * vector_tiles + TILES_PER_GATE
+        gamma_ih_at = 0
+        gamma_c_at = gamma_ih_at + vector_tiles
+        beta_c_at = gamma_c_at + TILES_PER_GATE
+        gamma_hh_at = beta_c_at + TILES_PER_GATE
         for vector, rows, at in (
+            (gamma_ih, gain_rows, gamma_ih_at),
+            (gamma_c, gain_rows, gamma_c_at),
+            (beta_c, gain_rows, beta_c_at),
             (gamma_hh, gain_rows, gamma_hh_at),
             (beta_hh, beta_rows, 0),
             (beta_ih, beta_rows, vector_tiles),
-            (gamma_c, gain_rows, gamma_c_at),
-            (beta_c, gain_rows, beta_c_at),
-            (gamma_ih, gain_rows, gamma_ih_at),
         ):
             as_rows = vector.rearrange("(r n) -> r n", n=P)
             nc.scalar.dma_start(out=rows[at : at + as_rows.shape[0], :], in_=as_rows)
@@ -200,7 +197,7 @@ def tile_layernormlstmcell_w_kernel(
         gain_columns = keep.tile([P, P], BF16, name="gain_columns")
         beta_columns = keep.tile([P, P], BF16, name="beta_columns")
         for rows, columns in ((gain_rows, gain_columns), (beta_rows, beta_columns)):
-            flipped_rows = turned.tile([P, P], BF16, name="flipped_rows", tag="turned")
+            flipped_rows = turned.tile([P, P], BF16, name="flipped_rows", tag="narrow")
             nc.tensor.transpose(flipped_rows[:], rows[:], ident_bf16[:])
             nc.vector.tensor_copy(out=columns[:], in_=flipped_rows[:])
         beta_sum_columns = keep.tile([P, vector_tiles], F32, name="beta_sum_columns")
@@ -210,21 +207,42 @@ def tile_layernormlstmcell_w_kernel(
             in1=beta_columns[:, vector_tiles : 2 * vector_tiles],
         )
 
-        gain_hh = keep.tile([P, G], BF16, name="gain_hh")
-        gain_ih = keep.tile([P, G], BF16, name="gain_ih")
-        beta_sum = keep.tile([P, G], F32, name="beta_sum")
-        gain_c = keep.tile([P, H], BF16, name="gain_c")
-        bias_c = keep.tile([P, H], BF16, name="bias_c")
-        spread(nc, turned, ident_bf16, gain_columns, gamma_c_at, gain_c[:])
-        spread(nc, turned, ident_bf16, gain_columns, beta_c_at, bias_c[:])
+        def new_banks():
+            return [sums.tile([P, BANK], F32, name="bank%d" % j, tag="sum") for j in range(BANKS_PER_GATE)]
 
+        def flat(bank):
+            return bank[:].rearrange("p m n -> p (m n)")
+
+        gain_hh = keep.tile([P, G], BF16, name="gain_hh")
+        beta_sum = keep.tile([P, G], F32, name="beta_sum")
+        for s in range(G // BANK):
+            beta_bank = turned.tile([P, PIECE_TILES, P], F32, name="beta_bank", tag="wide")
+            spread(nc, beta_bank, ident_f32, beta_sum_columns, s * PIECE_TILES)
+            if s % 2 == 0:
+                nc.vector.tensor_copy(out=beta_sum[:, s * BANK : (s + 1) * BANK], in_=flat(beta_bank))
+                gain_bank = turned.tile([P, LATE_TILES, P], BF16, name="gain_bank", tag="narrow")
+                spread(nc, gain_bank, ident_bf16, gain_columns, gamma_hh_at + s * PIECE_TILES)
+                nc.scalar.copy(out=gain_hh[:, s * BANK : (s + 2) * BANK], in_=flat(gain_bank))
+            else:
+                nc.scalar.copy(out=beta_sum[:, s * BANK : (s + 1) * BANK], in_=flat(beta_bank))
+
+        late = keep.tile([P, G + 2 * H], BF16, name="late")
+        gain_ih = late[:, gamma_ih_at * P : gamma_c_at * P]
+        gain_c = late[:, gamma_c_at * P : beta_c_at * P]
+        bias_c = late[:, beta_c_at * P : gamma_hh_at * P]
+        late_banks_per_gate = gamma_hh_at // LATE_TILES // (GATES - 1)
         rest = keep.tile([P, G], F32, name="rest")
         hh_stats = keep.tile([P, G // BANK, 6], F32, name="hh_stats")
         for gate in range(GATES):
-            cols = slice(gate * H, (gate + 1) * H)
-            spread(nc, turned, ident_bf16, gain_columns, gamma_hh_at + gate * TILES_PER_GATE, gain_hh[:, cols])
-            spread(nc, turned, ident_f32, beta_sum_columns, gate * TILES_PER_GATE, beta_sum[:, cols])
-            project_gate(nc, slabs, sums, W_hh_words, hh_planes, h_codes, h_scales, h_groups, gate, rest, hh_stats)
+            banks = new_banks()
+            for g in range(h_groups):
+                multiply_slab(nc, slabs, W_hh_words, hh_planes, h_codes, h_scales, h_groups, gate, g, banks)
+            move_out(nc, banks, gate, rest, hh_stats)
+            if gate < GATES - 1:
+                for s in range(gate * late_banks_per_gate, (gate + 1) * late_banks_per_gate):
+                    late_bank = turned.tile([P, LATE_TILES, P], BF16, name="late_bank", tag="narrow")
+                    spread(nc, late_bank, ident_bf16, gain_columns, s * LATE_TILES)
+                    nc.scalar.copy(out=late[:, s * LATE_TILES * P : (s + 1) * LATE_TILES * P], in_=flat(late_bank))
 
         mean_hh, rstd_hh = mean_and_rstd(nc, keep, minus_half, hh_stats, "hh")
         for gate in range(GATES):
@@ -237,9 +255,14 @@ def tile_layernormlstmcell_w_kernel(
         gates = keep.tile([P, G], F32, name="gates")
         ih_stats = keep.tile([P, G // BANK, 6], F32, name="ih_stats")
         for gate in range(GATES):
-            cols = slice(gate * H, (gate + 1) * H)
-            spread(nc, turned, ident_bf16, gain_columns, gamma_ih_at + gate * TILES_PER_GATE, gain_ih[:, cols])
-            project_gate(nc, slabs, sums, W_ih_words, ih_planes, x_codes, x_scales, x_groups, gate, gates, ih_stats)
+            banks = new_banks()
+            for g in range(x_groups):
+                multiply_slab(nc, slabs, W_ih_words, ih_planes, x_codes, x_scales, x_groups, gate, g, banks)
+            if gate < GATE_O:
+                move_out(nc, banks, gate, gates, ih_stats)
+        o_banks = banks
+        for j in range(BANKS_PER_GATE):
+            nc.vector.bn_stats(out=ih_stats[:, GATE_O * BANKS_PER_GATE + j, :], in_=o_banks[j][:])
         c_old = keep.tile([P, H], BF16, name="c_old")
         nc.sync.dma_start(out=c_old[:], in_=c_prev)
 
@@ -273,19 +296,22 @@ def tile_layernormlstmcell_w_kernel(
 
         mean_c = keep.tile([P, 1], F32, name="mean_c")
         nc.vector.tensor_scalar_mul(out=mean_c[:], in0=c_sum[:], scalar1=1.0 / H)
-        squares = keep.tile([P, H], F32, name="squares")
+        h_new = keep.tile([P, H], F32, name="h_new")
         square_sum = keep.tile([P, 1], F32, name="square_sum")
         nc.scalar.activation(
-            out=squares[:], in_=c_new[:], func=ACT.Square, bias=mean_c[:], scale=-1.0, accum_out=square_sum[:]
+            out=h_new[:], in_=c_new[:], func=ACT.Square, bias=mean_c[:], scale=-1.0, accum_out=square_sum[:]
         )
         rstd_c = inverse_root(nc, keep, minus_half, square_sum[:], 1.0 / H, "c")
-        centre(GATE_O)
+        for j in range(BANKS_PER_GATE):
+            cols = slice(GATE_O * H + j * BANK, GATE_O * H + (j + 1) * BANK)
+            nc.vector.scalar_tensor_tensor(
+                out=gates[:, cols], in0=o_banks[j][:], scalar=mean_ih, in1=gain_ih[:, cols], op0=ALU.subtract, op1=ALU.mult
+            )
         finish(GATE_O, ACT.Sigmoid)
 
         normed = keep.tile([P, H], F32, name="normed")
-        h_new = keep.tile([P, H], F32, name="h_new")
         nc.vector.scalar_tensor_tensor(
-            out=normed[:], in0=c_new[:], scalar=mean_c[:], in1=gain_c[:], op0=ALU.subtract, op1=ALU.mult
+            out=normed[:], in0=c_new[:], scalar=mean_c[:], in1=gain_c, op0=ALU.subtract, op1=ALU.mult
         )
         for j in range(BANKS_PER_GATE):
             cols = slice(j * BANK, (j + 1) * BANK)

@@ -61,7 +61,7 @@ def load_scale_planes(nc, keep, scales, groups, label):
     nc.vector.memset(plane_words, 0)
     source = scales.bitcast(I32)
     width = G // 4 // SCALE_CUTS
-    for quadrant in range(4):
+    for quadrant in (0, 2, 1, 3):
         for cut in range(SCALE_CUTS):
             cols = slice(cut * width, (cut + 1) * width)
             nc.sync.dma_start(
@@ -76,13 +76,17 @@ def spread(nc, bank, ident, columns, first):
         nc.tensor.transpose(bank[:, m, :], columns[:, first + m : first + m + 1].to_broadcast([P, P]), ident[:])
 
 
-def multiply_slab(nc, slabs, words, planes, codes, code_scales, groups, gate, g, banks):
+def multiply_slab(nc, slabs, words, planes, codes, code_scales, groups, gate, g, banks, loads=1):
     first = gate * H
     slab = slabs.tile([P, H], U32, name="slab", align_bytes=64)
-    nc.sync.dma_start(
-        out=slab[:].bitcast(I32),
-        in_=words[g, :, first : first + H, :].rearrange("p n t -> p (n t)").bitcast(I32),
-    )
+    width = H // loads
+    for part in range(loads):
+        nc.sync.dma_start(
+            out=slab[:, part * width : (part + 1) * width].bitcast(I32),
+            in_=words[g, :, first + part * width : first + (part + 1) * width, :]
+            .rearrange("p n t -> p (n t)")
+            .bitcast(I32),
+        )
     for j in range(BANKS_PER_GATE):
         nc.tensor.matmul_mx(
             out=banks[j][:],
@@ -257,7 +261,11 @@ def tile_layernormlstmcell_w_kernel(
         for gate in range(GATES):
             banks = new_banks()
             for g in range(x_groups):
-                multiply_slab(nc, slabs, W_ih_words, ih_planes, x_codes, x_scales, x_groups, gate, g, banks)
+                last_slab = gate == GATES - 1 and g == x_groups - 1
+                multiply_slab(
+                    nc, slabs, W_ih_words, ih_planes, x_codes, x_scales, x_groups, gate, g, banks,
+                    loads=BANKS_PER_GATE if last_slab else 1,
+                )
             if gate < GATE_O:
                 move_out(nc, banks, gate, gates, ih_stats)
         o_banks = banks
@@ -280,9 +288,9 @@ def tile_layernormlstmcell_w_kernel(
 
         centre(GATE_G)
         centre(GATE_I)
+        centre(GATE_F)
         finish(GATE_G, ACT.Tanh)
         finish(GATE_I, ACT.Sigmoid)
-        centre(GATE_F)
         finish(GATE_F, ACT.Sigmoid)
 
         c_new = keep.tile([P, H], F32, name="c_new")

@@ -39,7 +39,7 @@ def quantise_rows(nc, keep, turned, ident_f32, raw, groups, label):
     scales = keep.tile([P, groups, P], U8, name=label + "_scales", align_bytes=64)
     half = K_PASS // 2
     for g in range(groups):
-        flipped = turned.tile([P, 2, P], F32, name="flipped", tag="wide")
+        flipped = turned.tile([P, 2, P], F32, name="flipped", tag="turned")
         for u in range(2):
             nc.tensor.transpose(flipped[:, u, :], pairs[:, g * half + u : (g + 1) * half : 2], ident_f32[:])
         nc.vector.tensor_copy(
@@ -57,17 +57,16 @@ def quantise_rows(nc, keep, turned, ident_f32, raw, groups, label):
 
 def load_scale_planes(nc, keep, scales, groups, label):
     planes = keep.tile([P, G], U8, name=label, align_bytes=64)
-    plane_words = planes[:].bitcast(I32)
-    nc.vector.memset(plane_words, 0)
-    source = scales.bitcast(I32)
+    nc.vector.memset(planes[:].bitcast(I32), 0)
     width = G // 4 // SCALE_CUTS
-    for quadrant in (0, 2, 1, 3):
-        for cut in range(SCALE_CUTS):
-            cols = slice(cut * width, (cut + 1) * width)
-            nc.sync.dma_start(
-                out=plane_words[32 * quadrant : 32 * quadrant + 4 * groups, cols],
-                in_=source[:, 4 * quadrant : 4 * quadrant + 4, cols],
-            )
+    for cut in range(SCALE_CUTS):
+        cols = slice(cut * width, (cut + 1) * width)
+        for lower in range(2):
+            for queue, word, quadrant in ((nc.sync, I32, lower), (nc.scalar, F32, lower + 2)):
+                queue.dma_start(
+                    out=planes[:].bitcast(word)[32 * quadrant : 32 * quadrant + 4 * groups, cols],
+                    in_=scales.bitcast(word)[:, 4 * quadrant : 4 * quadrant + 4, cols],
+                )
     return planes
 
 
@@ -157,33 +156,7 @@ def tile_layernormlstmcell_w_kernel(
         keep = stack.enter_context(tc.tile_pool(name="keep", bufs=1))
         slabs = stack.enter_context(tc.tile_pool(name="slabs", bufs=SLAB_BUFS))
         sums = stack.enter_context(tc.psum_pool(name="sums", bufs=BANKS_PER_GATE + 1))
-        turned = stack.enter_context(tc.psum_pool(name="turned", bufs=2))
-
-        h_raw = keep.tile([P, H], BF16, name="h_raw")
-        nc.sync.dma_start(out=h_raw[:], in_=h_prev)
-        x_raw = keep.tile([P, IN], BF16, name="x_raw")
-        nc.sync.dma_start(out=x_raw[:], in_=x)
-        hh_planes = load_scale_planes(nc, keep, W_hh_scales, h_groups, "hh_planes")
-        ih_planes = load_scale_planes(nc, keep, W_ih_scales, x_groups, "ih_planes")
-
-        gain_rows = keep.tile([P, P], BF16, name="gain_rows")
-        beta_rows = keep.tile([P, P], BF16, name="beta_rows")
-        nc.vector.memset(gain_rows[:], 0.0)
-        nc.vector.memset(beta_rows[:], 0.0)
-        gamma_ih_at = 0
-        gamma_c_at = gamma_ih_at + vector_tiles
-        beta_c_at = gamma_c_at + TILES_PER_GATE
-        gamma_hh_at = beta_c_at + TILES_PER_GATE
-        for vector, rows, at in (
-            (gamma_ih, gain_rows, gamma_ih_at),
-            (gamma_c, gain_rows, gamma_c_at),
-            (beta_c, gain_rows, beta_c_at),
-            (gamma_hh, gain_rows, gamma_hh_at),
-            (beta_hh, beta_rows, 0),
-            (beta_ih, beta_rows, vector_tiles),
-        ):
-            as_rows = vector.rearrange("(r n) -> r n", n=P)
-            nc.scalar.dma_start(out=rows[at : at + as_rows.shape[0], :], in_=as_rows)
+        turned = stack.enter_context(tc.psum_pool(name="turned", bufs=4))
 
         ident_f32 = keep.tile([P, P], F32, name="ident_f32")
         make_identity(nc, ident_f32[:])
@@ -195,15 +168,47 @@ def tile_layernormlstmcell_w_kernel(
         nc.vector.memset(warm[:], 0.0)
         nc.scalar.activation(out=warm[:], in_=warm[:], func=ACT.Sigmoid)
 
+        h_raw = keep.tile([P, H], BF16, name="h_raw")
+        nc.sync.dma_start(out=h_raw[:], in_=h_prev)
+        x_raw = keep.tile([P, IN], BF16, name="x_raw")
+        nc.sync.dma_start(out=x_raw[:], in_=x)
+
+        def load_rows(queue, rows, at, vector):
+            as_rows = vector.rearrange("(r n) -> r n", n=P)
+            queue.dma_start(out=rows[at : at + as_rows.shape[0], :], in_=as_rows)
+
+        first_rows = keep.tile([P, P], BF16, name="first_rows")
+        beta_rows = keep.tile([P, P], BF16, name="beta_rows")
+        late_rows = keep.tile([P, P], BF16, name="late_rows")
+        for rows in (first_rows, beta_rows, late_rows):
+            nc.vector.memset(rows[:], 0.0)
+        load_rows(nc.scalar, first_rows, 0, gamma_hh)
+        load_rows(nc.scalar, beta_rows, 0, beta_hh)
+        load_rows(nc.scalar, beta_rows, vector_tiles, beta_ih)
+        hh_planes = load_scale_planes(nc, keep, W_hh_scales, h_groups, "hh_planes")
+        ih_planes = load_scale_planes(nc, keep, W_ih_scales, x_groups, "ih_planes")
+        gamma_ih_at = 0
+        gamma_c_at = gamma_ih_at + vector_tiles
+        beta_c_at = gamma_c_at + TILES_PER_GATE
+        late_tiles = beta_c_at + TILES_PER_GATE
+        load_rows(nc.sync, late_rows, gamma_ih_at, gamma_ih)
+        load_rows(nc.sync, late_rows, gamma_c_at, gamma_c)
+        load_rows(nc.sync, late_rows, beta_c_at, beta_c)
+
         h_codes, h_scales = quantise_rows(nc, keep, turned, ident_f32, h_raw, h_groups, "h")
         x_codes, x_scales = quantise_rows(nc, keep, turned, ident_f32, x_raw, x_groups, "x")
 
-        gain_columns = keep.tile([P, P], BF16, name="gain_columns")
+        first_columns = keep.tile([P, P], BF16, name="first_columns")
         beta_columns = keep.tile([P, P], BF16, name="beta_columns")
-        for rows, columns in ((gain_rows, gain_columns), (beta_rows, beta_columns)):
-            flipped_rows = turned.tile([P, P], BF16, name="flipped_rows", tag="narrow")
+        late_columns = keep.tile([P, P], BF16, name="late_columns")
+
+        def stand_up(rows, columns):
+            flipped_rows = turned.tile([P, P], BF16, name="flipped_rows", tag="turned")
             nc.tensor.transpose(flipped_rows[:], rows[:], ident_bf16[:])
             nc.vector.tensor_copy(out=columns[:], in_=flipped_rows[:])
+
+        stand_up(first_rows, first_columns)
+        stand_up(beta_rows, beta_columns)
         beta_sum_columns = keep.tile([P, vector_tiles], F32, name="beta_sum_columns")
         nc.vector.tensor_add(
             out=beta_sum_columns[:],
@@ -218,23 +223,16 @@ def tile_layernormlstmcell_w_kernel(
             return bank[:].rearrange("p m n -> p (m n)")
 
         gain_hh = keep.tile([P, G], BF16, name="gain_hh")
-        beta_sum = keep.tile([P, G], F32, name="beta_sum")
-        for s in range(G // BANK):
-            beta_bank = turned.tile([P, PIECE_TILES, P], F32, name="beta_bank", tag="wide")
-            spread(nc, beta_bank, ident_f32, beta_sum_columns, s * PIECE_TILES)
+        wide_bank = LATE_TILES * P
+        for s in range(G // wide_bank):
+            gain_bank = turned.tile([P, LATE_TILES, P], BF16, name="gain_bank", tag="turned")
+            spread(nc, gain_bank, ident_bf16, first_columns, s * LATE_TILES)
             if s % 2 == 0:
-                nc.vector.tensor_copy(out=beta_sum[:, s * BANK : (s + 1) * BANK], in_=flat(beta_bank))
-                gain_bank = turned.tile([P, LATE_TILES, P], BF16, name="gain_bank", tag="narrow")
-                spread(nc, gain_bank, ident_bf16, gain_columns, gamma_hh_at + s * PIECE_TILES)
-                nc.scalar.copy(out=gain_hh[:, s * BANK : (s + 2) * BANK], in_=flat(gain_bank))
+                nc.scalar.copy(out=gain_hh[:, s * wide_bank : (s + 1) * wide_bank], in_=flat(gain_bank))
             else:
-                nc.scalar.copy(out=beta_sum[:, s * BANK : (s + 1) * BANK], in_=flat(beta_bank))
+                nc.vector.tensor_copy(out=gain_hh[:, s * wide_bank : (s + 1) * wide_bank], in_=flat(gain_bank))
 
-        late = keep.tile([P, G + 2 * H], BF16, name="late")
-        gain_ih = late[:, gamma_ih_at * P : gamma_c_at * P]
-        gain_c = late[:, gamma_c_at * P : beta_c_at * P]
-        bias_c = late[:, beta_c_at * P : gamma_hh_at * P]
-        late_banks_per_gate = gamma_hh_at // LATE_TILES // (GATES - 1)
+        beta_sum = keep.tile([P, G], F32, name="beta_sum")
         rest = keep.tile([P, G], F32, name="rest")
         hh_stats = keep.tile([P, G // BANK, 6], F32, name="hh_stats")
         for gate in range(GATES):
@@ -242,11 +240,11 @@ def tile_layernormlstmcell_w_kernel(
             for g in range(h_groups):
                 multiply_slab(nc, slabs, W_hh_words, hh_planes, h_codes, h_scales, h_groups, gate, g, banks)
             move_out(nc, banks, gate, rest, hh_stats)
-            if gate < GATES - 1:
-                for s in range(gate * late_banks_per_gate, (gate + 1) * late_banks_per_gate):
-                    late_bank = turned.tile([P, LATE_TILES, P], BF16, name="late_bank", tag="narrow")
-                    spread(nc, late_bank, ident_bf16, gain_columns, s * LATE_TILES)
-                    nc.scalar.copy(out=late[:, s * LATE_TILES * P : (s + 1) * LATE_TILES * P], in_=flat(late_bank))
+            for s in range(gate * BANKS_PER_GATE, (gate + 1) * BANKS_PER_GATE):
+                beta_bank = turned.tile([P, PIECE_TILES, P], F32, name="beta_bank", tag="turned")
+                spread(nc, beta_bank, ident_f32, beta_sum_columns, s * PIECE_TILES)
+                nc.vector.tensor_copy(out=beta_sum[:, s * BANK : (s + 1) * BANK], in_=flat(beta_bank))
+        stand_up(late_rows, late_columns)
 
         mean_hh, rstd_hh = mean_and_rstd(nc, keep, minus_half, hh_stats, "hh")
         for gate in range(GATES):
@@ -256,6 +254,11 @@ def tile_layernormlstmcell_w_kernel(
             cols = slice(gate * H, (gate + 1) * H)
             scale_and_add(nc, rest[:, cols], rstd_hh, beta_sum[:, cols])
 
+        late = keep.tile([P, G + 2 * H], BF16, name="late")
+        gain_ih = late[:, gamma_ih_at * P : gamma_c_at * P]
+        gain_c = late[:, gamma_c_at * P : beta_c_at * P]
+        bias_c = late[:, beta_c_at * P : late_tiles * P]
+        late_banks_per_gate = late_tiles // LATE_TILES // (GATES - 1)
         gates = keep.tile([P, G], F32, name="gates")
         ih_stats = keep.tile([P, G // BANK, 6], F32, name="ih_stats")
         for gate in range(GATES):
@@ -268,6 +271,10 @@ def tile_layernormlstmcell_w_kernel(
                 )
             if gate < GATE_O:
                 move_out(nc, banks, gate, gates, ih_stats)
+                for s in range(gate * late_banks_per_gate, (gate + 1) * late_banks_per_gate):
+                    late_bank = turned.tile([P, LATE_TILES, P], BF16, name="late_bank", tag="turned")
+                    spread(nc, late_bank, ident_bf16, late_columns, s * LATE_TILES)
+                    nc.scalar.copy(out=late[:, s * wide_bank : (s + 1) * wide_bank], in_=flat(late_bank))
         o_banks = banks
         for j in range(BANKS_PER_GATE):
             nc.vector.bn_stats(out=ih_stats[:, GATE_O * BANKS_PER_GATE + j, :], in_=o_banks[j][:])

@@ -55,9 +55,16 @@ def quantise_rows(nc, keep, turned, ident_f32, raw, groups, label):
     return codes, scales
 
 
-def load_scale_planes(nc, keep, scales, groups, label):
+def load_scale_planes(nc, keep, scales, groups, label, beside):
     planes = keep.tile([P, G], U8, name=label, align_bytes=64)
     nc.vector.memset(planes[:].bitcast(I32), 0)
+    if beside:
+        for quadrant in range(4):
+            nc.gpsimd.dma_start(
+                out=planes[:].bitcast(F32)[32 * quadrant : 32 * quadrant + 4 * groups, :],
+                in_=scales.bitcast(F32)[:, 4 * quadrant : 4 * quadrant + 4, :],
+            )
+        return planes
     width = G // 4 // SCALE_CUTS
     for cut in range(SCALE_CUTS):
         cols = slice(cut * width, (cut + 1) * width)
@@ -185,8 +192,8 @@ def tile_layernormlstmcell_w_kernel(
         load_rows(nc.scalar, first_rows, 0, gamma_hh)
         load_rows(nc.scalar, beta_rows, 0, beta_hh)
         load_rows(nc.scalar, beta_rows, vector_tiles, beta_ih)
-        hh_planes = load_scale_planes(nc, keep, W_hh_scales, h_groups, "hh_planes")
-        ih_planes = load_scale_planes(nc, keep, W_ih_scales, x_groups, "ih_planes")
+        hh_planes = load_scale_planes(nc, keep, W_hh_scales, h_groups, "hh_planes", False)
+        ih_planes = load_scale_planes(nc, keep, W_ih_scales, x_groups, "ih_planes", True)
         gamma_ih_at = 0
         gamma_c_at = gamma_ih_at + vector_tiles
         beta_c_at = gamma_c_at + TILES_PER_GATE

@@ -26,7 +26,6 @@ TILES_PER_GATE = H // P
 EPS = 1e-5
 PIECE_TILES = BANK // P
 LATE_TILES = 2 * PIECE_TILES
-SCALE_CUTS = 2
 SLAB_BUFS = 10
 
 FLOPS = 2 * P * (IN + H) * G
@@ -55,25 +54,24 @@ def quantise_rows(nc, keep, turned, ident_f32, raw, groups, label):
     return codes, scales
 
 
-def load_scale_planes(nc, keep, scales, groups, label, beside):
+def load_scale_planes(nc, keep, scales, groups, label, front):
     planes = keep.tile([P, G], U8, name=label, align_bytes=64)
     nc.vector.memset(planes[:].bitcast(I32), 0)
-    if beside:
-        for quadrant in range(4):
-            nc.gpsimd.dma_start(
-                out=planes[:].bitcast(F32)[32 * quadrant : 32 * quadrant + 4 * groups, :],
-                in_=scales.bitcast(F32)[:, 4 * quadrant : 4 * quadrant + 4, :],
+    cut = front // 4
+    for quadrant in range(4):
+        rows = slice(32 * quadrant, 32 * quadrant + 4 * groups)
+        if front:
+            queue, word = ((nc.sync, I32), (nc.scalar, F32))[quadrant // 2]
+            queue.dma_start(
+                out=planes[:].bitcast(word)[rows, 0:cut],
+                in_=scales.bitcast(word)[:, 4 * quadrant : 4 * quadrant + 4, 0:cut],
             )
-        return planes
-    width = G // 4 // SCALE_CUTS
-    for cut in range(SCALE_CUTS):
-        cols = slice(cut * width, (cut + 1) * width)
-        for lower in range(2):
-            for queue, word, quadrant in ((nc.sync, I32, lower), (nc.scalar, F32, lower + 2)):
-                queue.dma_start(
-                    out=planes[:].bitcast(word)[32 * quadrant : 32 * quadrant + 4 * groups, cols],
-                    in_=scales.bitcast(word)[:, 4 * quadrant : 4 * quadrant + 4, cols],
-                )
+    for quadrant in range(4):
+        rows = slice(32 * quadrant, 32 * quadrant + 4 * groups)
+        nc.gpsimd.dma_start(
+            out=planes[:].bitcast(F32)[rows, cut : G // 4],
+            in_=scales.bitcast(F32)[:, 4 * quadrant : 4 * quadrant + 4, cut : G // 4],
+        )
     return planes
 
 
@@ -192,8 +190,8 @@ def tile_layernormlstmcell_w_kernel(
         load_rows(nc.scalar, first_rows, 0, gamma_hh)
         load_rows(nc.scalar, beta_rows, 0, beta_hh)
         load_rows(nc.scalar, beta_rows, vector_tiles, beta_ih)
-        hh_planes = load_scale_planes(nc, keep, W_hh_scales, h_groups, "hh_planes", False)
-        ih_planes = load_scale_planes(nc, keep, W_ih_scales, x_groups, "ih_planes", True)
+        hh_planes = load_scale_planes(nc, keep, W_hh_scales, h_groups, "hh_planes", H)
+        ih_planes = load_scale_planes(nc, keep, W_ih_scales, x_groups, "ih_planes", 0)
         gamma_ih_at = 0
         gamma_c_at = gamma_ih_at + vector_tiles
         beta_c_at = gamma_c_at + TILES_PER_GATE

@@ -28,6 +28,9 @@ PIECE_TILES = BANK // P
 LATE_TILES = 2 * PIECE_TILES
 SLAB_BUFS = 10
 
+EARLY = GATE_O * H
+IH_ROW, HH_ROW, BETA_ROW = 0, 4, 8
+
 FLOPS = 2 * P * (IN + H) * G
 
 
@@ -110,9 +113,12 @@ def move_out(nc, banks, gate, dest, stats):
         nc.vector.bn_stats(out=stats[:, gate * BANKS_PER_GATE + j, :], in_=dest[:, cols])
 
 
-def inverse_root(nc, keep, minus_half, total, share, label):
+def inverse_root(nc, keep, minus_half, total, share, label, on_scalar):
     shifted = keep.tile([P, 1], F32, name=label + "_shifted")
-    nc.gpsimd.tensor_scalar(out=shifted[:], in0=total, scalar1=share, scalar2=EPS, op0=ALU.mult, op1=ALU.add)
+    if on_scalar:
+        nc.scalar.activation(out=shifted[:], in_=total, func=ACT.Copy, scale=share, bias=EPS)
+    else:
+        nc.vector.tensor_scalar(out=shifted[:], in0=total, scalar1=share, scalar2=EPS, op0=ALU.mult, op1=ALU.add)
     rstd = keep.tile([P, 1], F32, name=label + "_rstd")
     nc.gpsimd.tensor_tensor(out=rstd[:], in0=shifted[:], in1=minus_half[:], op=ALU.pow)
     return rstd
@@ -121,8 +127,30 @@ def inverse_root(nc, keep, minus_half, total, share, label):
 def mean_and_rstd(nc, keep, minus_half, stats, label):
     mean_var = keep.tile([P, 2], F32, name=label + "_mean_var")
     nc.vector.bn_aggr(out=mean_var[:], in_=stats[:].rearrange("p c s -> p (c s)"))
-    rstd = inverse_root(nc, keep, minus_half, mean_var[:, 1:2], 1.0, label)
+    rstd = inverse_root(nc, keep, minus_half, mean_var[:, 1:2], 1.0, label, False)
     return mean_var[:, 0:1], rstd[:]
+
+
+def split_in_three(nc, keep, mean, rstd, dest, label):
+    product = keep.tile([P, 1], F32, name=label + "_product")
+    nc.gpsimd.tensor_scalar(out=product[:], in0=mean, scalar1=rstd, scalar2=-1.0, op0=ALU.mult, op1=ALU.mult)
+    nc.gpsimd.tensor_copy(out=dest[:, 0:1], in_=product[:])
+    left = keep.tile([P, 1], F32, name=label + "_left")
+    nc.gpsimd.tensor_tensor(out=left[:], in0=product[:], in1=dest[:, 0:1], op=ALU.subtract)
+    nc.gpsimd.tensor_copy(out=dest[:, 1:2], in_=left[:])
+    nc.gpsimd.tensor_tensor(out=dest[:, 2:3], in0=left[:], in1=dest[:, 1:2], op=ALU.subtract)
+
+
+def split_in_three_fast(nc, keep, mean, rstd, dest, label):
+    minus_mean = keep.tile([P, 1], F32, name=label + "_minus_mean")
+    nc.vector.tensor_scalar_mul(out=minus_mean[:], in0=mean, scalar1=-1.0)
+    product = keep.tile([P, 1], F32, name=label + "_product")
+    left = keep.tile([P, 1], F32, name=label + "_left")
+    nc.scalar.activation(out=dest[:, 0:1], in_=rstd, func=ACT.Copy, scale=minus_mean[:])
+    nc.scalar.activation(out=product[:], in_=rstd, func=ACT.Copy, scale=minus_mean[:])
+    nc.scalar.activation(out=dest[:, 1:2], in_=dest[:, 0:1], func=ACT.Identity, scale=-1.0, bias=product[:])
+    nc.scalar.activation(out=left[:], in_=dest[:, 0:1], func=ACT.Identity, scale=-1.0, bias=product[:])
+    nc.scalar.activation(out=dest[:, 2:3], in_=dest[:, 1:2], func=ACT.Identity, scale=-1.0, bias=left[:])
 
 
 def centre_and_gain(nc, values, mean, gain):
@@ -221,6 +249,20 @@ def tile_layernormlstmcell_w_kernel(
             in1=beta_columns[:, vector_tiles : 2 * vector_tiles],
         )
 
+        vector_rows = keep.tile([P, EARLY], BF16, name="vector_rows")
+        nc.vector.memset(vector_rows[:], 0.0)
+        nc.gpsimd.dma_start(out=vector_rows[IH_ROW : IH_ROW + 4, :], in_=gamma_ih[0:EARLY].partition_broadcast(4))
+        nc.gpsimd.dma_start(out=vector_rows[HH_ROW : HH_ROW + 4, :], in_=gamma_hh[0:EARLY].partition_broadcast(4))
+        nc.gpsimd.dma_start(
+            out=vector_rows[BETA_ROW : BETA_ROW + 1, :], in_=beta_ih[0:EARLY].rearrange("(o n) -> o n", o=1)
+        )
+        nc.gpsimd.dma_start(
+            out=vector_rows[BETA_ROW + 1 : BETA_ROW + 2, :], in_=beta_hh[0:EARLY].rearrange("(o n) -> o n", o=1)
+        )
+        factors = keep.tile([P, P], BF16, name="factors")
+        nc.vector.memset(factors[:], 0.0)
+        nc.vector.memset(factors[:, BETA_ROW : BETA_ROW + 2], 1.0)
+
         def new_banks():
             return [sums.tile([P, BANK], F32, name="bank%d" % j, tag="sum") for j in range(BANKS_PER_GATE)]
 
@@ -237,27 +279,48 @@ def tile_layernormlstmcell_w_kernel(
             else:
                 nc.vector.tensor_copy(out=gain_hh[:, s * wide_bank : (s + 1) * wide_bank], in_=flat(gain_bank))
 
-        beta_sum = keep.tile([P, G], F32, name="beta_sum")
+        bias_o = keep.tile([P, H], F32, name="bias_o")
         rest = keep.tile([P, G], F32, name="rest")
         hh_stats = keep.tile([P, G // BANK, 6], F32, name="hh_stats")
         for gate in range(GATES):
+            cols = slice(gate * H, (gate + 1) * H)
             banks = new_banks()
             for g in range(h_groups):
                 multiply_slab(nc, slabs, W_hh_words, hh_planes, h_codes, h_scales, h_groups, gate, g, banks)
             move_out(nc, banks, gate, rest, hh_stats)
-            for s in range(gate * BANKS_PER_GATE, (gate + 1) * BANKS_PER_GATE):
-                beta_bank = turned.tile([P, PIECE_TILES, P], F32, name="beta_bank", tag="turned")
-                spread(nc, beta_bank, ident_f32, beta_sum_columns, s * PIECE_TILES)
-                nc.vector.tensor_copy(out=beta_sum[:, s * BANK : (s + 1) * BANK], in_=flat(beta_bank))
+            if gate < GATE_O:
+                nc.vector.tensor_mul(out=rest[:, cols], in0=rest[:, cols], in1=gain_hh[:, cols])
+            if gate == 0:
+                for j in range(BANKS_PER_GATE):
+                    beta_bank = turned.tile([P, PIECE_TILES, P], F32, name="beta_bank", tag="turned")
+                    spread(nc, beta_bank, ident_f32, beta_sum_columns, (GATE_O * BANKS_PER_GATE + j) * PIECE_TILES)
+                    nc.scalar.copy(out=bias_o[:, j * BANK : (j + 1) * BANK], in_=flat(beta_bank))
         stand_up(late_rows, late_columns)
 
         mean_hh, rstd_hh = mean_and_rstd(nc, keep, minus_half, hh_stats, "hh")
-        for gate in range(GATES):
+        o_cols = slice(GATE_O * H, G)
+        centre_and_gain(nc, rest[:, o_cols], mean_hh, gain_hh[:, o_cols])
+        split_in_three(nc, keep, mean_hh, rstd_hh, factors[:, HH_ROW : HH_ROW + 3], "hh")
+        high = keep.tile([P, EARLY], BF16, name="high")
+        low = keep.tile([P, EARLY], BF16, name="low")
+
+        def upper(gate):
             cols = slice(gate * H, (gate + 1) * H)
-            centre_and_gain(nc, rest[:, cols], mean_hh, gain_hh[:, cols])
-        for gate in range(GATES):
+            nc.vector.tensor_scalar_mul(out=high[:, cols], in0=rest[:, cols], scalar1=rstd_hh)
+
+        def lower(gate):
             cols = slice(gate * H, (gate + 1) * H)
-            scale_and_add(nc, rest[:, cols], rstd_hh, beta_sum[:, cols])
+            nc.vector.scalar_tensor_tensor(
+                out=low[:, cols], in0=rest[:, cols], scalar=rstd_hh, in1=high[:, cols], op0=ALU.mult, op1=ALU.subtract
+            )
+
+        upper(0)
+        upper(1)
+        lower(0)
+        upper(2)
+        lower(1)
+        lower(2)
+        scale_and_add(nc, rest[:, o_cols], rstd_hh, bias_o[:])
 
         late = keep.tile([P, G + 2 * H], BF16, name="late")
         gain_ih = late[:, gamma_ih_at * P : gamma_c_at * P]
@@ -267,6 +330,7 @@ def tile_layernormlstmcell_w_kernel(
         gates = keep.tile([P, G], F32, name="gates")
         ih_stats = keep.tile([P, G // BANK, 6], F32, name="ih_stats")
         for gate in range(GATES):
+            cols = slice(gate * H, (gate + 1) * H)
             banks = new_banks()
             for g in range(x_groups):
                 last_slab = gate == GATES - 1 and g == x_groups - 1
@@ -280,30 +344,62 @@ def tile_layernormlstmcell_w_kernel(
                     late_bank = turned.tile([P, LATE_TILES, P], BF16, name="late_bank", tag="turned")
                     spread(nc, late_bank, ident_bf16, late_columns, s * LATE_TILES)
                     nc.scalar.copy(out=late[:, s * wide_bank : (s + 1) * wide_bank], in_=flat(late_bank))
+                nc.vector.tensor_mul(out=gates[:, cols], in0=gates[:, cols], in1=gain_ih[:, cols])
         o_banks = banks
         for j in range(BANKS_PER_GATE):
             nc.vector.bn_stats(out=ih_stats[:, GATE_O * BANKS_PER_GATE + j, :], in_=o_banks[j][:])
         c_old = keep.tile([P, H], BF16, name="c_old")
         nc.sync.dma_start(out=c_old[:], in_=c_prev)
 
+        order = [(gate, j) for gate in (GATE_G, GATE_I, GATE_F) for j in range(BANKS_PER_GATE)]
+        funcs = {GATE_G: ACT.Tanh, GATE_I: ACT.Sigmoid, GATE_F: ACT.Sigmoid}
+        added = []
+
+        def piece(q):
+            gate, j = order[q]
+            return slice(gate * H + j * BANK, gate * H + (j + 1) * BANK)
+
+        def begin(q, pool, tag):
+            bank = pool.tile([P, BANK], F32, name="added%d" % q, tag=tag)
+            nc.tensor.matmul(out=bank[:], lhsT=ident_bf16[:], rhs=high[:, piece(q)], start=True, stop=False)
+            nc.tensor.matmul(out=bank[:], lhsT=ident_bf16[:], rhs=low[:, piece(q)], start=False, stop=False)
+            added.append(bank)
+
+        def close(q):
+            nc.tensor.matmul(out=added[q][:], lhsT=factor_rows[:], rhs=vector_rows[:, piece(q)], start=False, stop=True)
+
+        for q in range(3):
+            begin(q, turned, "turned")
+        begin(3, sums, "sum")
         mean_ih, rstd_ih = mean_and_rstd(nc, keep, minus_half, ih_stats, "ih")
+        split_in_three_fast(nc, keep, mean_ih, rstd_ih, factors[:, IH_ROW : IH_ROW + 3], "ih")
+        for j in range(BANKS_PER_GATE):
+            cols = slice(GATE_O * H + j * BANK, GATE_O * H + (j + 1) * BANK)
+            nc.vector.scalar_tensor_tensor(
+                out=gates[:, cols], in0=o_banks[j][:], scalar=mean_ih, in1=gain_ih[:, cols], op0=ALU.subtract, op1=ALU.mult
+            )
+        for q in range(4, 7):
+            begin(q, sums, "sum")
+        flipped_factors = turned.tile([P, P], BF16, name="flipped_factors", tag="turned")
+        nc.tensor.transpose(flipped_factors[:], factors[:], ident_bf16[:])
+        factor_rows = keep.tile([P, P], BF16, name="factor_rows")
+        nc.scalar.copy(out=factor_rows[:], in_=flipped_factors[:])
+        scale_and_add(nc, gates[:, o_cols], rstd_ih, rest[:, o_cols])
+        for q in range(7):
+            close(q)
+        for q in range(len(order)):
+            nc.vector.scalar_tensor_tensor(
+                out=gates[:, piece(q)], in0=gates[:, piece(q)], scalar=rstd_ih, in1=added[q][:], op0=ALU.mult, op1=ALU.add
+            )
+            nc.scalar.activation(out=gates[:, piece(q)], in_=gates[:, piece(q)], func=funcs[order[q][0]])
+            if q + 7 < len(order):
+                begin(q + 7, turned, "turned")
+                close(q + 7)
+
+        nc.scalar.activation(out=gates[:, o_cols], in_=gates[:, o_cols], func=ACT.Sigmoid)
 
         def block(gate):
             return gates[:, gate * H : (gate + 1) * H]
-
-        def centre(gate):
-            centre_and_gain(nc, block(gate), mean_ih, gain_ih[:, gate * H : (gate + 1) * H])
-
-        def finish(gate, func):
-            scale_and_add(nc, block(gate), rstd_ih, rest[:, gate * H : (gate + 1) * H])
-            nc.scalar.activation(out=block(gate), in_=block(gate), func=func)
-
-        centre(GATE_G)
-        centre(GATE_I)
-        centre(GATE_F)
-        finish(GATE_G, ACT.Tanh)
-        finish(GATE_I, ACT.Sigmoid)
-        finish(GATE_F, ACT.Sigmoid)
 
         c_new = keep.tile([P, H], F32, name="c_new")
         c_sum = keep.tile([P, 1], F32, name="c_sum")
@@ -321,18 +417,12 @@ def tile_layernormlstmcell_w_kernel(
         nc.scalar.activation(
             out=h_new[:], in_=c_new[:], func=ACT.Square, bias=mean_c[:], scale=-1.0, accum_out=square_sum[:]
         )
-        rstd_c = inverse_root(nc, keep, minus_half, square_sum[:], 1.0 / H, "c")
-        for j in range(BANKS_PER_GATE):
-            cols = slice(GATE_O * H + j * BANK, GATE_O * H + (j + 1) * BANK)
-            nc.vector.scalar_tensor_tensor(
-                out=gates[:, cols], in0=o_banks[j][:], scalar=mean_ih, in1=gain_ih[:, cols], op0=ALU.subtract, op1=ALU.mult
-            )
-        finish(GATE_O, ACT.Sigmoid)
-
+        rstd_c = inverse_root(nc, keep, minus_half, square_sum[:], 1.0 / H, "c", True)
         normed = keep.tile([P, H], F32, name="normed")
         nc.vector.scalar_tensor_tensor(
             out=normed[:], in0=c_new[:], scalar=mean_c[:], in1=gain_c, op0=ALU.subtract, op1=ALU.mult
         )
+
         for j in range(BANKS_PER_GATE):
             cols = slice(j * BANK, (j + 1) * BANK)
             scale_and_add(nc, normed[:, cols], rstd_c[:], bias_c[:, cols])

@@ -351,7 +351,7 @@ def tile_layernormlstmcell_w_kernel(
         c_old = keep.tile([P, H], BF16, name="c_old")
         nc.sync.dma_start(out=c_old[:], in_=c_prev)
 
-        order = [(gate, j) for gate in (GATE_G, GATE_I, GATE_F) for j in range(BANKS_PER_GATE)]
+        order = [(gate, j) for gate in (GATE_F, GATE_G, GATE_I) for j in range(BANKS_PER_GATE)]
         funcs = {GATE_G: ACT.Tanh, GATE_I: ACT.Sigmoid, GATE_F: ACT.Sigmoid}
         added = []
 
@@ -392,6 +392,9 @@ def tile_layernormlstmcell_w_kernel(
                 out=gates[:, piece(q)], in0=gates[:, piece(q)], scalar=rstd_ih, in1=added[q][:], op0=ALU.mult, op1=ALU.add
             )
             nc.scalar.activation(out=gates[:, piece(q)], in_=gates[:, piece(q)], func=funcs[order[q][0]])
+            if order[q][0] == GATE_F:
+                old = c_old[:, order[q][1] * BANK : (order[q][1] + 1) * BANK]
+                nc.gpsimd.tensor_tensor(out=gates[:, piece(q)], in0=gates[:, piece(q)], in1=old, op=ALU.mult)
             if q + 7 < len(order):
                 begin(q + 7, turned, "turned")
                 close(q + 7)
@@ -404,7 +407,6 @@ def tile_layernormlstmcell_w_kernel(
         c_new = keep.tile([P, H], F32, name="c_new")
         c_sum = keep.tile([P, 1], F32, name="c_sum")
         nc.vector.tensor_mul(out=block(GATE_I), in0=block(GATE_I), in1=block(GATE_G))
-        nc.vector.tensor_mul(out=block(GATE_F), in0=block(GATE_F), in1=c_old[:])
         nc.vector.scalar_tensor_tensor(
             out=c_new[:], in0=block(GATE_I), scalar=1.0, in1=block(GATE_F), op0=ALU.mult, op1=ALU.add, accum_out=c_sum[:]
         )

@@ -406,7 +406,9 @@ def tile_layernormlstmcell_w_kernel(
 
         c_new = keep.tile([P, H], F32, name="c_new")
         c_sum = keep.tile([P, 1], F32, name="c_sum")
-        nc.vector.tensor_mul(out=block(GATE_I), in0=block(GATE_I), in1=block(GATE_G))
+        for j in range(BANKS_PER_GATE):
+            cols = slice(j * BANK, (j + 1) * BANK)
+            nc.vector.tensor_mul(out=block(GATE_I)[:, cols], in0=block(GATE_I)[:, cols], in1=block(GATE_G)[:, cols])
         nc.vector.scalar_tensor_tensor(
             out=c_new[:], in0=block(GATE_I), scalar=1.0, in1=block(GATE_F), op0=ALU.mult, op1=ALU.add, accum_out=c_sum[:]
         )

@@ -306,7 +306,7 @@ def tile_layernormlstmcell_w_kernel(
 
         def upper(gate):
             cols = slice(gate * H, (gate + 1) * H)
-            nc.vector.tensor_scalar_mul(out=high[:, cols], in0=rest[:, cols], scalar1=rstd_hh)
+            nc.scalar.activation(out=high[:, cols], in_=rest[:, cols], func=ACT.Copy, scale=rstd_hh)
 
         def lower(gate):
             cols = slice(gate * H, (gate + 1) * H)
@@ -419,9 +419,9 @@ def tile_layernormlstmcell_w_kernel(
         h_new = keep.tile([P, H], F32, name="h_new")
         square_sum = keep.tile([P, 1], F32, name="square_sum")
         nc.scalar.activation(
-            out=h_new[:], in_=c_new[:], func=ACT.Square, bias=mean_c[:], scale=-1.0, accum_out=square_sum[:]
+            out=h_new[:], in_=c_new[:], func=ACT.Square, bias=c_sum[:], scale=-1.0 * H, accum_out=square_sum[:]
         )
-        rstd_c = inverse_root(nc, keep, minus_half, square_sum[:], 1.0 / H, "c", True)
+        rstd_c = inverse_root(nc, keep, minus_half, square_sum[:], 1.0 / (H * H * H), "c", True)
         normed = keep.tile([P, H], F32, name="normed")
         nc.vector.scalar_tensor_tensor(
             out=normed[:], in0=c_new[:], scalar=mean_c[:], in1=gain_c, op0=ALU.subtract, op1=ALU.mult

from contextlib import ExitStack

import concourse.mybir as mybir
from concourse.masks import make_identity

F32 = mybir.dt.float32
BF16 = mybir.dt.bfloat16
I32 = mybir.dt.int32
U32 = mybir.dt.uint32
U8 = mybir.dt.uint8
FP8X4 = mybir.dt.float8_e4m3fn_x4
ALU = mybir.AluOpType
ACT = mybir.ActivationFunctionType

P = 128
PACK = 4
K_PASS = P * PACK
BANK = 512
IN = 2048
H = 1536
GATES = 4
G = GATES * H
GATE_I, GATE_F, GATE_G, GATE_O = 0, 1, 2, 3
BANKS_PER_GATE = H // BANK
TILES_PER_GATE = H // P
EPS = 1e-5
PIECE_TILES = BANK // P
LATE_TILES = 2 * PIECE_TILES
SLAB_BUFS = 10

EARLY = GATE_O * H
IH_ROW, HH_ROW, BETA_ROW = 0, 4, 8

FLOPS = 2 * P * (IN + H) * G


def quantise_rows(nc, keep, turned, ident_f32, raw, groups, label):
    pairs = raw[:].bitcast(F32)
    grouped = keep.tile([P, groups, P, PACK], BF16, name=label + "_grouped", align_bytes=64)
    codes = keep.tile([P, groups, P], U32, name=label + "_codes", align_bytes=64)
    scales = keep.tile([P, groups, P], U8, name=label + "_scales", align_bytes=64)
    half = K_PASS // 2
    for g in range(groups):
        flipped = turned.tile([P, 2, P], F32, name="flipped", tag="turned")
        for u in range(2):
            nc.tensor.transpose(flipped[:, u, :], pairs[:, g * half + u : (g + 1) * half : 2], ident_f32[:])
        nc.vector.tensor_copy(
            out=grouped[:, g].rearrange("p b t -> p (b t)").bitcast(F32).rearrange("p (b u) -> p b u", u=2),
            in_=flipped[:].rearrange("p u b -> p b u"),
        )
    for g in range(groups):
        nc.vector.quantize_mx(
            out=codes[:, g, :].bitcast(FP8X4),
            scales=scales[:, g, :],
            in_=grouped[:, g].rearrange("p b t -> p (b t)"),
        )
    return codes, scales


def load_scale_planes(nc, keep, scales, groups, label, front):
    planes = keep.tile([P, G], U8, name=label, align_bytes=64)
    nc.vector.memset(planes[:].bitcast(I32), 0)
    cut = front // 4
    for quadrant in range(4):
        rows = slice(32 * quadrant, 32 * quadrant + 4 * groups)
        if front:
            queue, word = ((nc.sync, I32), (nc.scalar, F32))[quadrant // 2]
            queue.dma_start(
                out=planes[:].bitcast(word)[rows, 0:cut],
                in_=scales.bitcast(word)[:, 4 * quadrant : 4 * quadrant + 4, 0:cut],
            )
    for quadrant in range(4):
        rows = slice(32 * quadrant, 32 * quadrant + 4 * groups)
        nc.gpsimd.dma_start(
            out=planes[:].bitcast(F32)[rows, cut : G // 4],
            in_=scales.bitcast(F32)[:, 4 * quadrant : 4 * quadrant + 4, cut : G // 4],
        )
    return planes


def spread(nc, bank, ident, columns, first):
    for m in range(bank.shape[1]):
        nc.tensor.transpose(bank[:, m, :], columns[:, first + m : first + m + 1].to_broadcast([P, P]), ident[:])


def multiply_slab(nc, slabs, words, planes, codes, code_scales, groups, gate, g, banks, loads=1):
    first = gate * H
    slab = slabs.tile([P, H], U32, name="slab", align_bytes=64)
    width = H // loads
    for part in range(loads):
        nc.sync.dma_start(
            out=slab[:, part * width : (part + 1) * width].bitcast(I32),
            in_=words[g, :, first + part * width : first + (part + 1) * width, :]
            .rearrange("p n t -> p (n t)")
            .bitcast(I32),
        )
    for j in range(BANKS_PER_GATE):
        nc.tensor.matmul_mx(
            out=banks[j][:],
            lhsT=codes[:, g, :].bitcast(FP8X4),
            lhsT_scale=code_scales[:, g, :],
            rhs=slab[:, j * BANK : (j + 1) * BANK].bitcast(FP8X4),
            rhs_scale=planes[4 * g : P, first + j * BANK : first + (j + 1) * BANK],
            start=(g == 0),
            stop=(g == groups - 1),
        )


def move_out(nc, banks, gate, dest, stats):
    for j in range(BANKS_PER_GATE):
        cols = slice(gate * H + j * BANK, gate * H + (j + 1) * BANK)
        nc.scalar.copy(out=dest[:, cols], in_=banks[j][:])
        nc.vector.bn_stats(out=stats[:, gate * BANKS_PER_GATE + j, :], in_=dest[:, cols])


def inverse_root(nc, keep, minus_half, total, share, label, on_scalar):
    shifted = keep.tile([P, 1], F32, name=label + "_shifted")
    if on_scalar:
        nc.scalar.activation(out=shifted[:], in_=total, func=ACT.Copy, scale=share, bias=EPS)
    else:
        nc.vector.tensor_scalar(out=shifted[:], in0=total, scalar1=share, scalar2=EPS, op0=ALU.mult, op1=ALU.add)
    rstd = keep.tile([P, 1], F32, name=label + "_rstd")
    nc.gpsimd.tensor_tensor(out=rstd[:], in0=shifted[:], in1=minus_half[:], op=ALU.pow)
    return rstd


def mean_and_rstd(nc, keep, minus_half, stats, label):
    mean_var = keep.tile([P, 2], F32, name=label + "_mean_var")
    nc.vector.bn_aggr(out=mean_var[:], in_=stats[:].rearrange("p c s -> p (c s)"))
    rstd = inverse_root(nc, keep, minus_half, mean_var[:, 1:2], 1.0, label, False)
    return mean_var[:, 0:1], rstd[:]


def split_in_three(nc, keep, mean, rstd, dest, label):
    product = keep.tile([P, 1], F32, name=label + "_product")
    nc.gpsimd.tensor_scalar(out=product[:], in0=mean, scalar1=rstd, scalar2=-1.0, op0=ALU.mult, op1=ALU.mult)
    nc.gpsimd.tensor_copy(out=dest[:, 0:1], in_=product[:])
    left = keep.tile([P, 1], F32, name=label + "_left")
    nc.gpsimd.tensor_tensor(out=left[:], in0=product[:], in1=dest[:, 0:1], op=ALU.subtract)
    nc.gpsimd.tensor_copy(out=dest[:, 1:2], in_=left[:])
    nc.gpsimd.tensor_tensor(out=dest[:, 2:3], in0=left[:], in1=dest[:, 1:2], op=ALU.subtract)


def split_in_three_fast(nc, keep, mean, rstd, dest, label):
    minus_mean = keep.tile([P, 1], F32, name=label + "_minus_mean")
    nc.vector.tensor_scalar_mul(out=minus_mean[:], in0=mean, scalar1=-1.0)
    product = keep.tile([P, 1], F32, name=label + "_product")
    left = keep.tile([P, 1], F32, name=label + "_left")
    nc.scalar.activation(out=dest[:, 0:1], in_=rstd, func=ACT.Copy, scale=minus_mean[:])
    nc.scalar.activation(out=product[:], in_=rstd, func=ACT.Copy, scale=minus_mean[:])
    nc.scalar.activation(out=dest[:, 1:2], in_=dest[:, 0:1], func=ACT.Identity, scale=-1.0, bias=product[:])
    nc.scalar.activation(out=left[:], in_=dest[:, 0:1], func=ACT.Identity, scale=-1.0, bias=product[:])
    nc.scalar.activation(out=dest[:, 2:3], in_=dest[:, 1:2], func=ACT.Identity, scale=-1.0, bias=left[:])


def centre_and_gain(nc, values, mean, gain):
    nc.vector.scalar_tensor_tensor(out=values, in0=values, scalar=mean, in1=gain, op0=ALU.subtract, op1=ALU.mult)


def scale_and_add(nc, values, rstd, addend):
    nc.vector.scalar_tensor_tensor(out=values, in0=values, scalar=rstd, in1=addend, op0=ALU.mult, op1=ALU.add)


def tile_layernormlstmcell_w_kernel(
    tc,
    x,
    h_prev,
    c_prev,
    W_ih_words,
    W_ih_scales,
    W_hh_words,
    W_hh_scales,
    gamma_ih,
    beta_ih,
    gamma_hh,
    beta_hh,
    gamma_c,
    beta_c,
    out_0,
    out_1,
):
    nc = tc.nc
    x_groups = IN // K_PASS
    h_groups = H // K_PASS
    vector_tiles = G // P

    with ExitStack() as stack:
        stack.enter_context(tc.manual_schedule())
        keep = stack.enter_context(tc.tile_pool(name="keep", bufs=1))
        slabs = stack.enter_context(tc.tile_pool(name="slabs", bufs=SLAB_BUFS))
        sums = stack.enter_context(tc.psum_pool(name="sums", bufs=BANKS_PER_GATE + 1))
        turned = stack.enter_context(tc.psum_pool(name="turned", bufs=4))

        ident_f32 = keep.tile([P, P], F32, name="ident_f32")
        make_identity(nc, ident_f32[:])
        ident_bf16 = keep.tile([P, P], BF16, name="ident_bf16")
        make_identity(nc, ident_bf16[:])
        minus_half = keep.tile([P, 1], F32, name="minus_half")
        nc.gpsimd.memset(minus_half[:], -0.5)
        warm = keep.tile([P, 1], F32, name="warm")
        nc.vector.memset(warm[:], 0.0)
        nc.scalar.activation(out=warm[:], in_=warm[:], func=ACT.Sigmoid)

        h_raw = keep.tile([P, H], BF16, name="h_raw")
        nc.sync.dma_start(out=h_raw[:], in_=h_prev)
        x_raw = keep.tile([P, IN], BF16, name="x_raw")
        nc.sync.dma_start(out=x_raw[:], in_=x)

        def load_rows(queue, rows, at, vector):
            as_rows = vector.rearrange("(r n) -> r n", n=P)
            queue.dma_start(out=rows[at : at + as_rows.shape[0], :], in_=as_rows)

        first_rows = keep.tile([P, P], BF16, name="first_rows")
        beta_rows = keep.tile([P, P], BF16, name="beta_rows")
        late_rows = keep.tile([P, P], BF16, name="late_rows")
        for rows in (first_rows, beta_rows, late_rows):
            nc.vector.memset(rows[:], 0.0)
        load_rows(nc.scalar, first_rows, 0, gamma_hh)
        load_rows(nc.scalar, beta_rows, 0, beta_hh)
        load_rows(nc.scalar, beta_rows, vector_tiles, beta_ih)
        hh_planes = load_scale_planes(nc, keep, W_hh_scales, h_groups, "hh_planes", H)
        ih_planes = load_scale_planes(nc, keep, W_ih_scales, x_groups, "ih_planes", 0)
        gamma_ih_at = 0
        gamma_c_at = gamma_ih_at + vector_tiles
        beta_c_at = gamma_c_at + TILES_PER_GATE
        late_tiles = beta_c_at + TILES_PER_GATE
        load_rows(nc.sync, late_rows, gamma_ih_at, gamma_ih)
        load_rows(nc.sync, late_rows, gamma_c_at, gamma_c)
        load_rows(nc.sync, late_rows, beta_c_at, beta_c)

        h_codes, h_scales = quantise_rows(nc, keep, turned, ident_f32, h_raw, h_groups, "h")
        x_codes, x_scales = quantise_rows(nc, keep, turned, ident_f32, x_raw, x_groups, "x")

        first_columns = keep.tile([P, P], BF16, name="first_columns")
        beta_columns = keep.tile([P, P], BF16, name="beta_columns")
        late_columns = keep.tile([P, P], BF16, name="late_columns")

        def stand_up(rows, columns):
            flipped_rows = turned.tile([P, P], BF16, name="flipped_rows", tag="turned")
            nc.tensor.transpose(flipped_rows[:], rows[:], ident_bf16[:])
            nc.vector.tensor_copy(out=columns[:], in_=flipped_rows[:])

        stand_up(first_rows, first_columns)
        stand_up(beta_rows, beta_columns)
        beta_sum_columns = keep.tile([P, vector_tiles], F32, name="beta_sum_columns")
        nc.vector.tensor_add(
            out=beta_sum_columns[:],
            in0=beta_columns[:, 0:vector_tiles],
            in1=beta_columns[:, vector_tiles : 2 * vector_tiles],
        )

        vector_rows = keep.tile([P, EARLY], BF16, name="vector_rows")
        nc.vector.memset(vector_rows[:], 0.0)
        nc.gpsimd.dma_start(out=vector_rows[IH_ROW : IH_ROW + 4, :], in_=gamma_ih[0:EARLY].partition_broadcast(4))
        nc.gpsimd.dma_start(out=vector_rows[HH_ROW : HH_ROW + 4, :], in_=gamma_hh[0:EARLY].partition_broadcast(4))
        nc.gpsimd.dma_start(
            out=vector_rows[BETA_ROW : BETA_ROW + 1, :], in_=beta_ih[0:EARLY].rearrange("(o n) -> o n", o=1)
        )
        nc.gpsimd.dma_start(
            out=vector_rows[BETA_ROW + 1 : BETA_ROW + 2, :], in_=beta_hh[0:EARLY].rearrange("(o n) -> o n", o=1)
        )
        factors = keep.tile([P, P], BF16, name="factors")
        nc.vector.memset(factors[:], 0.0)
        nc.vector.memset(factors[:, BETA_ROW : BETA_ROW + 2], 1.0)

        def new_banks():
            return [sums.tile([P, BANK], F32, name="bank%d" % j, tag="sum") for j in range(BANKS_PER_GATE)]

        def flat(bank):
            return bank[:].rearrange("p m n -> p (m n)")

        gain_hh = keep.tile([P, G], BF16, name="gain_hh")
        wide_bank = LATE_TILES * P
        for s in range(G // wide_bank):
            gain_bank = turned.tile([P, LATE_TILES, P], BF16, name="gain_bank", tag="turned")
            spread(nc, gain_bank, ident_bf16, first_columns, s * LATE_TILES)
            if s % 2 == 0:
                nc.scalar.copy(out=gain_hh[:, s * wide_bank : (s + 1) * wide_bank], in_=flat(gain_bank))
            else:
                nc.vector.tensor_copy(out=gain_hh[:, s * wide_bank : (s + 1) * wide_bank], in_=flat(gain_bank))

        bias_o = keep.tile([P, H], F32, name="bias_o")
        rest = keep.tile([P, G], F32, name="rest")
        hh_stats = keep.tile([P, G // BANK, 6], F32, name="hh_stats")
        for gate in range(GATES):
            cols = slice(gate * H, (gate + 1) * H)
            banks = new_banks()
            for g in range(h_groups):
                multiply_slab(nc, slabs, W_hh_words, hh_planes, h_codes, h_scales, h_groups, gate, g, banks)
            move_out(nc, banks, gate, rest, hh_stats)
            if gate < GATE_O:
                nc.vector.tensor_mul(out=rest[:, cols], in0=rest[:, cols], in1=gain_hh[:, cols])
            if gate == 0:
                for j in range(BANKS_PER_GATE):
                    beta_bank = turned.tile([P, PIECE_TILES, P], F32, name="beta_bank", tag="turned")
                    spread(nc, beta_bank, ident_f32, beta_sum_columns, (GATE_O * BANKS_PER_GATE + j) * PIECE_TILES)
                    nc.scalar.copy(out=bias_o[:, j * BANK : (j + 1) * BANK], in_=flat(beta_bank))
        stand_up(late_rows, late_columns)

        mean_hh, rstd_hh = mean_and_rstd(nc, keep, minus_half, hh_stats, "hh")
        o_cols = slice(GATE_O * H, G)
        centre_and_gain(nc, rest[:, o_cols], mean_hh, gain_hh[:, o_cols])
        split_in_three(nc, keep, mean_hh, rstd_hh, factors[:, HH_ROW : HH_ROW + 3], "hh")
        high = keep.tile([P, EARLY], BF16, name="high")
        low = keep.tile([P, EARLY], BF16, name="low")

        def upper(gate):
            cols = slice(gate * H, (gate + 1) * H)
            nc.scalar.activation(out=high[:, cols], in_=rest[:, cols], func=ACT.Copy, scale=rstd_hh)

        def lower(gate):
            cols = slice(gate * H, (gate + 1) * H)
            nc.vector.scalar_tensor_tensor(
                out=low[:, cols], in0=rest[:, cols], scalar=rstd_hh, in1=high[:, cols], op0=ALU.mult, op1=ALU.subtract
            )

        upper(0)
        upper(1)
        lower(0)
        upper(2)
        lower(1)
        lower(2)
        scale_and_add(nc, rest[:, o_cols], rstd_hh, bias_o[:])

        late = keep.tile([P, G + 2 * H], BF16, name="late")
        gain_ih = late[:, gamma_ih_at * P : gamma_c_at * P]
        gain_c = late[:, gamma_c_at * P : beta_c_at * P]
        bias_c = late[:, beta_c_at * P : late_tiles * P]
        late_banks_per_gate = late_tiles // LATE_TILES // (GATES - 1)
        gates = keep.tile([P, G], F32, name="gates")
        ih_stats = keep.tile([P, G // BANK, 6], F32, name="ih_stats")
        for gate in range(GATES):
            cols = slice(gate * H, (gate + 1) * H)
            banks = new_banks()
            for g in range(x_groups):
                last_slab = gate == GATES - 1 and g == x_groups - 1
                multiply_slab(
                    nc, slabs, W_ih_words, ih_planes, x_codes, x_scales, x_groups, gate, g, banks,
                    loads=BANKS_PER_GATE if last_slab else 1,
                )
            if gate < GATE_O:
                move_out(nc, banks, gate, gates, ih_stats)
                for s in range(gate * late_banks_per_gate, (gate + 1) * late_banks_per_gate):
                    late_bank = turned.tile([P, LATE_TILES, P], BF16, name="late_bank", tag="turned")
                    spread(nc, late_bank, ident_bf16, late_columns, s * LATE_TILES)
                    nc.scalar.copy(out=late[:, s * wide_bank : (s + 1) * wide_bank], in_=flat(late_bank))
                nc.vector.tensor_mul(out=gates[:, cols], in0=gates[:, cols], in1=gain_ih[:, cols])
        o_banks = banks
        for j in range(BANKS_PER_GATE):
            nc.vector.bn_stats(out=ih_stats[:, GATE_O * BANKS_PER_GATE + j, :], in_=o_banks[j][:])
        c_old = keep.tile([P, H], BF16, name="c_old")
        nc.sync.dma_start(out=c_old[:], in_=c_prev)

        order = [(gate, j) for gate in (GATE_F, GATE_G, GATE_I) for j in range(BANKS_PER_GATE)]
        funcs = {GATE_G: ACT.Tanh, GATE_I: ACT.Sigmoid, GATE_F: ACT.Sigmoid}
        added = []

        def piece(q):
            gate, j = order[q]
            return slice(gate * H + j * BANK, gate * H + (j + 1) * BANK)

        def begin(q, pool, tag):
            bank = pool.tile([P, BANK], F32, name="added%d" % q, tag=tag)
            nc.tensor.matmul(out=bank[:], lhsT=ident_bf16[:], rhs=high[:, piece(q)], start=True, stop=False)
            nc.tensor.matmul(out=bank[:], lhsT=ident_bf16[:], rhs=low[:, piece(q)], start=False, stop=False)
            added.append(bank)

        def close(q):
            nc.tensor.matmul(out=added[q][:], lhsT=factor_rows[:], rhs=vector_rows[:, piece(q)], start=False, stop=True)

        for q in range(3):
            begin(q, turned, "turned")
        begin(3, sums, "sum")
        mean_ih, rstd_ih = mean_and_rstd(nc, keep, minus_half, ih_stats, "ih")
        split_in_three_fast(nc, keep, mean_ih, rstd_ih, factors[:, IH_ROW : IH_ROW + 3], "ih")
        for j in range(BANKS_PER_GATE):
            cols = slice(GATE_O * H + j * BANK, GATE_O * H + (j + 1) * BANK)
            nc.vector.scalar_tensor_tensor(
                out=gates[:, cols], in0=o_banks[j][:], scalar=mean_ih, in1=gain_ih[:, cols], op0=ALU.subtract, op1=ALU.mult
            )
        for q in range(4, 7):
            begin(q, sums, "sum")
        flipped_factors = turned.tile([P, P], BF16, name="flipped_factors", tag="turned")
        nc.tensor.transpose(flipped_factors[:], factors[:], ident_bf16[:])
        factor_rows = keep.tile([P, P], BF16, name="factor_rows")
        nc.scalar.copy(out=factor_rows[:], in_=flipped_factors[:])
        scale_and_add(nc, gates[:, o_cols], rstd_ih, rest[:, o_cols])
        for q in range(7):
            close(q)
        for q in range(len(order)):
            nc.vector.scalar_tensor_tensor(
                out=gates[:, piece(q)], in0=gates[:, piece(q)], scalar=rstd_ih, in1=added[q][:], op0=ALU.mult, op1=ALU.add
            )
            nc.scalar.activation(out=gates[:, piece(q)], in_=gates[:, piece(q)], func=funcs[order[q][0]])
            if order[q][0] == GATE_F:
                old = c_old[:, order[q][1] * BANK : (order[q][1] + 1) * BANK]
                nc.gpsimd.tensor_tensor(out=gates[:, piece(q)], in0=gates[:, piece(q)], in1=old, op=ALU.mult)
            if q + 7 < len(order):
                begin(q + 7, turned, "turned")
                close(q + 7)

        nc.scalar.activation(out=gates[:, o_cols], in_=gates[:, o_cols], func=ACT.Sigmoid)

        def block(gate):
            return gates[:, gate * H : (gate + 1) * H]

        c_new = keep.tile([P, H], F32, name="c_new")
        c_sum = keep.tile([P, 1], F32, name="c_sum")
        for j in range(BANKS_PER_GATE):
            cols = slice(j * BANK, (j + 1) * BANK)
            nc.vector.tensor_mul(out=block(GATE_I)[:, cols], in0=block(GATE_I)[:, cols], in1=block(GATE_G)[:, cols])
        nc.vector.scalar_tensor_tensor(
            out=c_new[:], in0=block(GATE_I), scalar=1.0, in1=block(GATE_F), op0=ALU.mult, op1=ALU.add, accum_out=c_sum[:]
        )
        nc.sync.dma_start(out=out_1, in_=c_new[:])

        mean_c = keep.tile([P, 1], F32, name="mean_c")
        nc.vector.tensor_scalar_mul(out=mean_c[:], in0=c_sum[:], scalar1=1.0 / H)
        h_new = keep.tile([P, H], F32, name="h_new")
        square_sum = keep.tile([P, 1], F32, name="square_sum")
        nc.scalar.activation(
            out=h_new[:], in_=c_new[:], func=ACT.Square, bias=c_sum[:], scale=-1.0 * H, accum_out=square_sum[:]
        )
        rstd_c = inverse_root(nc, keep, minus_half, square_sum[:], 1.0 / (H * H * H), "c", True)
        normed = keep.tile([P, H], F32, name="normed")
        nc.vector.scalar_tensor_tensor(
            out=normed[:], in0=c_new[:], scalar=mean_c[:], in1=gain_c, op0=ALU.subtract, op1=ALU.mult
        )

        for j in range(BANKS_PER_GATE):
            cols = slice(j * BANK, (j + 1) * BANK)
            scale_and_add(nc, normed[:, cols], rstd_c[:], bias_c[:, cols])
            nc.scalar.activation(out=normed[:, cols], in_=normed[:, cols], func=ACT.Tanh)
        for j in range(BANKS_PER_GATE):
            cols = slice(j * BANK, (j + 1) * BANK)
            nc.vector.tensor_mul(out=h_new[:, cols], in0=block(GATE_O)[:, cols], in1=normed[:, cols])
            nc.sync.dma_start(out=out_0[:, cols], in_=h_new[:, cols])
